import numpy as np
import ml_dtypes


def mxq(x, axis, fmt="e4m3"):
    dtype, down = {"e4m3": (ml_dtypes.float8_e4m3fn, 7), "e5m2": (ml_dtypes.float8_e5m2, 14)}[fmt]
    v = np.moveaxis(np.asarray(x, np.float32).astype(ml_dtypes.bfloat16).astype(np.float64), axis, -1)
    blocks = v.reshape(v.shape[:-1] + (-1, 32))
    amax = np.abs(blocks).max(-1, keepdims=True)
    byte = np.maximum(np.where(amax > 0, np.frexp(amax)[1] - 1 + 127, 0) - down, 1)
    scale = np.exp2(byte - 127.0)
    codes = (blocks / scale).astype(np.float32).astype(dtype).astype(np.float64)
    return np.moveaxis((codes * scale).reshape(v.shape), -1, axis)


WIDE = False


def mx_kscale(k):
    if not WIDE:
        return np.ones(k)
    levels = np.array([20, -20, 10, -10, 0])
    a = np.random.permutation(np.resize(levels, k // 512 * 4)).reshape(k // 512, 4)
    idx = np.arange(k)
    return np.exp2(a[idx // 512, idx % 128 // 32])


BF16 = ml_dtypes.bfloat16


def bf(x):
    return np.asarray(x, np.float32).astype(BF16)


def f64(x):
    return np.asarray(x).astype(np.float64)


B, N, D, H, K = 8, 64, 256, 512, 16384
NT = B * N
LN2PI_2 = np.log(2.0 * np.pi) / 2.0


def setup_inputs():
    s = mx_kscale(K)
    cent = 0.4 * np.random.standard_normal((B, D))
    idx = np.random.randint(0, B, K)
    xf = np.repeat(cent, N, axis=0) + 0.5 * np.random.standard_normal((NT, D))
    mean = 0.6 * cent[idx] + 0.1 * np.random.standard_normal((K, D))
    var = 0.35 * np.exp(0.2 * np.random.standard_normal((K, D))) * s[:, None]
    g = np.random.standard_normal((NT, K)) * np.exp2(np.random.randint(-12, 1, (NT, 1))) * s[None, :]
    return {"xf": bf(xf), "mean": bf(mean), "var": bf(var), "grad_out": bf(g)}


def reference(xf, mean, var, grad_out):
    xv, mv, vv = f64(xf), f64(mean), f64(var)
    inv_var = 1.0 / vv
    gq = mxq(f64(grad_out), 1, "e5m2")
    a = gq @ mxq(mv * inv_var, 0, "e4m3")
    b = gq @ mxq(inv_var, 0, "e4m3")
    return a - xv * b

@@ -1,0 +1,153 @@
+from contextlib import ExitStack
+
+import concourse.mybir as mybir
+from concourse.masks import make_identity
+
+F32 = mybir.dt.float32
+BF16 = mybir.dt.bfloat16
+U32 = mybir.dt.uint32
+U8 = mybir.dt.uint8
+E4M3_X4 = mybir.dt.float8_e4m3fn_x4
+E5M2_X4 = mybir.dt.float8_e5m2_x4
+ACT = mybir.ActivationFunctionType
+ALU = mybir.AluOpType
+
+P = 128
+PACK = 4
+K_PASS = P * PACK
+
+NT, D, K = 512, 256, 16384
+N_TILES = NT // P
+PASSES_PER_ROUND = 2
+K_ROUND = PASSES_PER_ROUND * K_PASS
+ROUNDS = K // K_ROUND
+WORDS_PER_PASS = K_PASS // 2
+TILES_PER_BANK = 2
+BANKS_PER_PASS = N_TILES // TILES_PER_BANK
+VECTOR_EVERY = 4
+
+FLOPS = 2 * NT * K * (2 * D)
+
+
+def tile_gaussianmlpbasislayer_pb_k_kernel(tc, xf, mean, var, grad_out, out):
+    nc = tc.nc
+    with ExitStack() as ctx:
+        const = ctx.enter_context(tc.tile_pool(name="const", bufs=1))
+        loads = ctx.enter_context(tc.tile_pool(name="loads", bufs=4))
+        work = ctx.enter_context(tc.tile_pool(name="work", bufs=2))
+        packed = ctx.enter_context(tc.tile_pool(name="packed", bufs=3))
+        acc_pool = ctx.enter_context(tc.psum_pool(name="acc", bufs=1))
+        xt_pool = ctx.enter_context(tc.psum_pool(name="xt", bufs=4))
+
+        identity = const.tile([P, P], F32)
+        make_identity(nc, identity[:])
+
+        acc = [acc_pool.tile([P, 2 * D], F32, name="acc%d" % a) for a in range(N_TILES)]
+
+        for r in range(ROUNDS):
+            k_rows = slice(r * K_ROUND, (r + 1) * K_ROUND)
+
+            var_sb = loads.tile([P, PASSES_PER_ROUND, PACK, D], BF16)
+            nc.sync.dma_start(
+                out=var_sb[:].rearrange("p c j d -> p c (j d)"),
+                in_=var[k_rows, :].rearrange("(c p j) d -> p c (j d)", p=P, j=PACK),
+            )
+            g_sb = loads.tile([P, N_TILES, K_ROUND], BF16)
+            nc.sync.dma_start(
+                out=g_sb[:], in_=grad_out[:, k_rows].rearrange("(a p) k -> p a k", p=P)
+            )
+            mean_sb = loads.tile([P, PASSES_PER_ROUND, PACK, D], BF16)
+            nc.sync.dma_start(
+                out=mean_sb[:].rearrange("p c j d -> p c (j d)"),
+                in_=mean[k_rows, :].rearrange("(c p j) d -> p c (j d)", p=P, j=PACK),
+            )
+
+            rsqrt_var = work.tile([P, PASSES_PER_ROUND, D, PACK], F32)
+            nc.scalar.activation(
+                out=rsqrt_var[:],
+                in_=var_sb[:].rearrange("p c j d -> p c d j"),
+                func=ACT.Abs_reciprocal_sqrt,
+            )
+            inv_var = work.tile([P, PASSES_PER_ROUND, D, PACK], F32)
+            nc.scalar.activation(out=inv_var[:], in_=rsqrt_var[:], func=ACT.Square)
+
+            g_words = g_sb[:].bitcast(F32)
+            g_bf = work.tile([P, PASSES_PER_ROUND, N_TILES, P, PACK], BF16, align_bytes=64)
+            g_bf_words = g_bf[:].bitcast(F32)
+            for c in range(PASSES_PER_ROUND):
+                for h in range(BANKS_PER_PASS):
+                    xt = xt_pool.tile([P, TILES_PER_BANK, 2, P], F32)
+                    for i in range(TILES_PER_BANK):
+                        for u in range(2):
+                            first = c * WORDS_PER_PASS + u
+                            nc.tensor.transpose(
+                                out=xt[:, i, u, :],
+                                in_=g_words[
+                                    :,
+                                    h * TILES_PER_BANK + i,
+                                    first : (c + 1) * WORDS_PER_PASS : 2,
+                                ],
+                                identity=identity[:],
+                            )
+                    tiles = slice(h * TILES_PER_BANK, (h + 1) * TILES_PER_BANK)
+                    bank = c * BANKS_PER_PASS + h
+                    if bank % VECTOR_EVERY == VECTOR_EVERY - 1:
+                        nc.vector.tensor_copy(
+                            out=g_bf_words[:, c, tiles],
+                            in_=xt[:].rearrange("p i u n -> p i n u"),
+                        )
+                    else:
+                        nc.scalar.copy(
+                            out=g_bf_words[:, c, tiles],
+                            in_=xt[:].rearrange("p i u n -> p i n u"),
+                        )
+
+            w_bf = work.tile([P, PASSES_PER_ROUND, 2, D, PACK], BF16, align_bytes=64)
+            nc.vector.tensor_tensor(
+                out=w_bf[:, :, 0],
+                in0=mean_sb[:].rearrange("p c j d -> p c d j"),
+                in1=inv_var[:],
+                op=ALU.mult,
+            )
+            nc.vector.tensor_copy(out=w_bf[:, :, 1], in_=inv_var[:])
+
+            g_codes = packed.tile([P, PASSES_PER_ROUND, NT], U32, align_bytes=64)
+            g_scales = packed.tile([P, PASSES_PER_ROUND, NT], U8, align_bytes=64)
+            nc.vector.quantize_mx(
+                out=g_codes[:].rearrange("p c n -> p (c n)").bitcast(E5M2_X4),
+                scales=g_scales[:].rearrange("p c n -> p (c n)"),
+                in_=g_bf[:].rearrange("p c a n t -> p (c a n t)"),
+            )
+            w_codes = packed.tile([P, PASSES_PER_ROUND, 2 * D], U32, align_bytes=64)
+            w_scales = packed.tile([P, PASSES_PER_ROUND, 2 * D], U8, align_bytes=64)
+            nc.vector.quantize_mx(
+                out=w_codes[:].rearrange("p c w -> p (c w)").bitcast(E4M3_X4),
+                scales=w_scales[:].rearrange("p c w -> p (c w)"),
+                in_=w_bf[:].rearrange("p c h d t -> p (c h d t)"),
+            )
+
+            for c in range(PASSES_PER_ROUND):
+                for a in range(N_TILES):
+                    rows = slice(a * P, (a + 1) * P)
+                    nc.tensor.matmul_mx(
+                        out=acc[a][:],
+                        lhsT=g_codes[:, c, rows].bitcast(E5M2_X4),
+                        lhsT_scale=g_scales[:, c, rows],
+                        rhs=w_codes[:, c, :].bitcast(E4M3_X4),
+                        rhs_scale=w_scales[:, c, :],
+                        start=(r == 0 and c == 0),
+                        stop=(r == ROUNDS - 1 and c == PASSES_PER_ROUND - 1),
+                    )
+
+        x_sb = const.tile([P, N_TILES, D], BF16)
+        nc.sync.dma_start(out=x_sb[:], in_=xf.rearrange("(a p) d -> p a d", p=P))
+        for a in range(N_TILES):
+            x_b = work.tile([P, D], F32)
+            nc.vector.tensor_tensor(
+                out=x_b[:], in0=x_sb[:, a, :], in1=acc[a][:, D : 2 * D], op=ALU.mult
+            )
+            result = work.tile([P, D], F32)
+            nc.vector.tensor_tensor(
+                out=result[:], in0=acc[a][:, 0:D], in1=x_b[:], op=ALU.subtract
+            )
+            nc.sync.dma_start(out=out[a * P : (a + 1) * P, :], in_=result[:])

@@ -18,12 +18,17 @@ K_PASS = P * PACK
 
 NT, D, K = 512, 256, 16384
 N_TILES = NT // P
-PASSES_PER_ROUND = 2
-K_ROUND = PASSES_PER_ROUND * K_PASS
-ROUNDS = K // K_ROUND
+PASSES = K // K_PASS
 WORDS_PER_PASS = K_PASS // 2
 TILES_PER_BANK = 2
 BANKS_PER_PASS = N_TILES // TILES_PER_BANK
+
+PASSES_PER_LOAD = 2
+K_LOAD = PASSES_PER_LOAD * K_PASS
+LOADS = K // K_LOAD
+LOAD_BUFS = 4
+LOADS_AHEAD = LOAD_BUFS - 1
+
 VECTOR_EVERY = 4
 
 FLOPS = 2 * NT * K * (2 * D)
@@ -33,120 +38,154 @@ def tile_gaussianmlpbasislayer_pb_k_kernel(tc, xf, mean, var, grad_out, out):
     nc = tc.nc
     with ExitStack() as ctx:
         const = ctx.enter_context(tc.tile_pool(name="const", bufs=1))
-        loads = ctx.enter_context(tc.tile_pool(name="loads", bufs=4))
-        work = ctx.enter_context(tc.tile_pool(name="work", bufs=2))
-        packed = ctx.enter_context(tc.tile_pool(name="packed", bufs=3))
+        loads = ctx.enter_context(tc.tile_pool(name="loads", bufs=LOAD_BUFS))
+        pairs = ctx.enter_context(tc.tile_pool(name="pairs", bufs=2))
+        triples = ctx.enter_context(tc.tile_pool(name="triples", bufs=3))
         acc_pool = ctx.enter_context(tc.psum_pool(name="acc", bufs=1))
-        xt_pool = ctx.enter_context(tc.psum_pool(name="xt", bufs=4))
+        xt_pool = ctx.enter_context(tc.psum_pool(name="xt", bufs=2 * BANKS_PER_PASS))
+        ctx.enter_context(tc.manual_schedule())
 
         identity = const.tile([P, P], F32)
         make_identity(nc, identity[:])
 
         acc = [acc_pool.tile([P, 2 * D], F32, name="acc%d" % a) for a in range(N_TILES)]
 
-        for r in range(ROUNDS):
-            k_rows = slice(r * K_ROUND, (r + 1) * K_ROUND)
+        var_sb, mean_sb, g_sb = {}, {}, {}
+        rsqrt_var, inv_var, xt, g_bf = {}, {}, {}, {}
+        g_codes, g_scales, w_codes, w_scales = {}, {}, {}, {}
 
-            var_sb = loads.tile([P, PASSES_PER_ROUND, PACK, D], BF16)
-            nc.sync.dma_start(
-                out=var_sb[:].rearrange("p c j d -> p c (j d)"),
-                in_=var[k_rows, :].rearrange("(c p j) d -> p c (j d)", p=P, j=PACK),
-            )
-            g_sb = loads.tile([P, N_TILES, K_ROUND], BF16)
-            nc.sync.dma_start(
-                out=g_sb[:], in_=grad_out[:, k_rows].rearrange("(a p) k -> p a k", p=P)
-            )
-            mean_sb = loads.tile([P, PASSES_PER_ROUND, PACK, D], BF16)
-            nc.sync.dma_start(
-                out=mean_sb[:].rearrange("p c j d -> p c (j d)"),
-                in_=mean[k_rows, :].rearrange("(c p j) d -> p c (j d)", p=P, j=PACK),
-            )
+        def load(i, pieces):
+            var_sb[i] = loads.tile([P, PASSES_PER_LOAD, PACK, D], BF16, name="var_sb")
+            g_sb[i] = loads.tile([P, N_TILES, K_LOAD], BF16, name="g_sb")
+            mean_sb[i] = loads.tile([P, PASSES_PER_LOAD, PACK, D], BF16, name="mean_sb")
+            n = PASSES_PER_LOAD // pieces
+            for piece in range(pieces):
+                cs = slice(piece * n, (piece + 1) * n)
+                ks = slice(piece * n * K_PASS, (piece + 1) * n * K_PASS)
+                k_rows = slice((i * PASSES_PER_LOAD + piece * n) * K_PASS, (i * PASSES_PER_LOAD + (piece + 1) * n) * K_PASS)
+                nc.sync.dma_start(
+                    out=var_sb[i][:, cs].rearrange("p c j d -> p c (j d)"),
+                    in_=var[k_rows, :].rearrange("(c p j) d -> p c (j d)", p=P, j=PACK),
+                )
+                nc.sync.dma_start(
+                    out=g_sb[i][:, :, ks],
+                    in_=grad_out[:, k_rows].rearrange("(a p) k -> p a k", p=P),
+                )
+                nc.sync.dma_start(
+                    out=mean_sb[i][:, cs].rearrange("p c j d -> p c (j d)"),
+                    in_=mean[k_rows, :].rearrange("(c p j) d -> p c (j d)", p=P, j=PACK),
+                )
 
-            rsqrt_var = work.tile([P, PASSES_PER_ROUND, D, PACK], F32)
+        def transpose_g(c):
+            i, ci = divmod(c, PASSES_PER_LOAD)
+            g_words = g_sb[i][:].bitcast(F32)
+            for h in range(BANKS_PER_PASS):
+                xt[c, h] = xt_pool.tile([P, TILES_PER_BANK, 2, P], F32, name="xt")
+                for b in range(TILES_PER_BANK):
+                    for u in range(2):
+                        nc.tensor.transpose(
+                            out=xt[c, h][:, b, u, :],
+                            in_=g_words[
+                                :,
+                                h * TILES_PER_BANK + b,
+                                ci * WORDS_PER_PASS + u : (ci + 1) * WORDS_PER_PASS : 2,
+                            ],
+                            identity=identity[:],
+                        )
+
+        def empty_bank(c, h):
+            if h == 0:
+                g_bf[c] = triples.tile([P, N_TILES, P, PACK], BF16, name="g_bf", align_bytes=64)
+            g_bf_words = g_bf[c][:].bitcast(F32)
+            dst = g_bf_words[:, h * TILES_PER_BANK : (h + 1) * TILES_PER_BANK]
+            src = xt[c, h][:].rearrange("p b u n -> p b n u")
+            if (c * BANKS_PER_PASS + h) % VECTOR_EVERY == VECTOR_EVERY - 1:
+                nc.vector.tensor_copy(out=dst, in_=src)
+            else:
+                nc.scalar.copy(out=dst, in_=src)
+
+        def take_rsqrt(c):
+            i, ci = divmod(c, PASSES_PER_LOAD)
+            rsqrt_var[c] = pairs.tile([P, D, PACK], F32, name="rsqrt_var")
             nc.scalar.activation(
-                out=rsqrt_var[:],
-                in_=var_sb[:].rearrange("p c j d -> p c d j"),
+                out=rsqrt_var[c][:],
+                in_=var_sb[i][:, ci].rearrange("p j d -> p d j"),
                 func=ACT.Abs_reciprocal_sqrt,
             )
-            inv_var = work.tile([P, PASSES_PER_ROUND, D, PACK], F32)
-            nc.scalar.activation(out=inv_var[:], in_=rsqrt_var[:], func=ACT.Square)
 
-            g_words = g_sb[:].bitcast(F32)
-            g_bf = work.tile([P, PASSES_PER_ROUND, N_TILES, P, PACK], BF16, align_bytes=64)
-            g_bf_words = g_bf[:].bitcast(F32)
-            for c in range(PASSES_PER_ROUND):
-                for h in range(BANKS_PER_PASS):
-                    xt = xt_pool.tile([P, TILES_PER_BANK, 2, P], F32)
-                    for i in range(TILES_PER_BANK):
-                        for u in range(2):
-                            first = c * WORDS_PER_PASS + u
-                            nc.tensor.transpose(
-                                out=xt[:, i, u, :],
-                                in_=g_words[
-                                    :,
-                                    h * TILES_PER_BANK + i,
-                                    first : (c + 1) * WORDS_PER_PASS : 2,
-                                ],
-                                identity=identity[:],
-                            )
-                    tiles = slice(h * TILES_PER_BANK, (h + 1) * TILES_PER_BANK)
-                    bank = c * BANKS_PER_PASS + h
-                    if bank % VECTOR_EVERY == VECTOR_EVERY - 1:
-                        nc.vector.tensor_copy(
-                            out=g_bf_words[:, c, tiles],
-                            in_=xt[:].rearrange("p i u n -> p i n u"),
-                        )
-                    else:
-                        nc.scalar.copy(
-                            out=g_bf_words[:, c, tiles],
-                            in_=xt[:].rearrange("p i u n -> p i n u"),
-                        )
+        def square(c):
+            inv_var[c] = triples.tile([P, D, PACK], F32, name="inv_var")
+            nc.scalar.activation(out=inv_var[c][:], in_=rsqrt_var[c][:], func=ACT.Square)
 
-            w_bf = work.tile([P, PASSES_PER_ROUND, 2, D, PACK], BF16, align_bytes=64)
+        def quantise(c):
+            i, ci = divmod(c, PASSES_PER_LOAD)
+            w_bf = pairs.tile([P, 2, D, PACK], BF16, name="w_bf", align_bytes=64)
             nc.vector.tensor_tensor(
-                out=w_bf[:, :, 0],
-                in0=mean_sb[:].rearrange("p c j d -> p c d j"),
-                in1=inv_var[:],
+                out=w_bf[:, 0],
+                in0=mean_sb[i][:, ci].rearrange("p j d -> p d j"),
+                in1=inv_var[c][:],
                 op=ALU.mult,
             )
-            nc.vector.tensor_copy(out=w_bf[:, :, 1], in_=inv_var[:])
-
-            g_codes = packed.tile([P, PASSES_PER_ROUND, NT], U32, align_bytes=64)
-            g_scales = packed.tile([P, PASSES_PER_ROUND, NT], U8, align_bytes=64)
+            nc.vector.tensor_copy(out=w_bf[:, 1], in_=inv_var[c][:])
+            g_codes[c] = triples.tile([P, NT], U32, name="g_codes", align_bytes=64)
+            g_scales[c] = triples.tile([P, NT], U8, name="g_scales", align_bytes=64)
             nc.vector.quantize_mx(
-                out=g_codes[:].rearrange("p c n -> p (c n)").bitcast(E5M2_X4),
-                scales=g_scales[:].rearrange("p c n -> p (c n)"),
-                in_=g_bf[:].rearrange("p c a n t -> p (c a n t)"),
+                out=g_codes[c][:].bitcast(E5M2_X4),
+                scales=g_scales[c][:],
+                in_=g_bf[c][:].rearrange("p a n t -> p (a n t)"),
             )
-            w_codes = packed.tile([P, PASSES_PER_ROUND, 2 * D], U32, align_bytes=64)
-            w_scales = packed.tile([P, PASSES_PER_ROUND, 2 * D], U8, align_bytes=64)
+            w_codes[c] = triples.tile([P, 2 * D], U32, name="w_codes", align_bytes=64)
+            w_scales[c] = triples.tile([P, 2 * D], U8, name="w_scales", align_bytes=64)
             nc.vector.quantize_mx(
-                out=w_codes[:].rearrange("p c w -> p (c w)").bitcast(E4M3_X4),
-                scales=w_scales[:].rearrange("p c w -> p (c w)"),
-                in_=w_bf[:].rearrange("p c h d t -> p (c h d t)"),
+                out=w_codes[c][:].bitcast(E4M3_X4),
+                scales=w_scales[c][:],
+                in_=w_bf[:].rearrange("p h d t -> p (h d t)"),
             )
 
-            for c in range(PASSES_PER_ROUND):
-                for a in range(N_TILES):
-                    rows = slice(a * P, (a + 1) * P)
-                    nc.tensor.matmul_mx(
-                        out=acc[a][:],
-                        lhsT=g_codes[:, c, rows].bitcast(E5M2_X4),
-                        lhsT_scale=g_scales[:, c, rows],
-                        rhs=w_codes[:, c, :].bitcast(E4M3_X4),
-                        rhs_scale=w_scales[:, c, :],
-                        start=(r == 0 and c == 0),
-                        stop=(r == ROUNDS - 1 and c == PASSES_PER_ROUND - 1),
-                    )
+        def multiply(c):
+            for a in range(N_TILES):
+                rows = slice(a * P, (a + 1) * P)
+                nc.tensor.matmul_mx(
+                    out=acc[a][:],
+                    lhsT=g_codes[c][:, rows].bitcast(E5M2_X4),
+                    lhsT_scale=g_scales[c][:, rows],
+                    rhs=w_codes[c][:].bitcast(E4M3_X4),
+                    rhs_scale=w_scales[c][:],
+                    start=(c == 0),
+                    stop=(c == PASSES - 1),
+                )
 
+        load(0, PASSES_PER_LOAD)
+        for i in range(1, LOADS_AHEAD):
+            load(i, 1)
         x_sb = const.tile([P, N_TILES, D], BF16)
         nc.sync.dma_start(out=x_sb[:], in_=xf.rearrange("(a p) d -> p a d", p=P))
+
+        for step in range(-2, PASSES + 1):
+            if step >= 0 and step % PASSES_PER_LOAD == 0:
+                i = step // PASSES_PER_LOAD + LOADS_AHEAD
+                if i < LOADS:
+                    load(i, 1)
+            if step + 2 < PASSES:
+                transpose_g(step + 2)
+            if 0 <= step - 1:
+                multiply(step - 1)
+            if 0 <= step + 1 < PASSES:
+                square(step + 1)
+                empty_bank(step + 1, 0)
+            if step + 2 < PASSES:
+                take_rsqrt(step + 2)
+            if 0 <= step < PASSES:
+                quantise(step)
+            if 0 <= step + 1 < PASSES:
+                empty_bank(step + 1, 1)
+
         for a in range(N_TILES):
-            x_b = work.tile([P, D], F32)
+            x_b = pairs.tile([P, D], F32, name="x_b")
             nc.vector.tensor_tensor(
                 out=x_b[:], in0=x_sb[:, a, :], in1=acc[a][:, D : 2 * D], op=ALU.mult
             )
-            result = work.tile([P, D], F32)
+            result = pairs.tile([P, D], F32, name="result")
             nc.vector.tensor_tensor(
                 out=result[:], in0=acc[a][:, 0:D], in1=x_b[:], op=ALU.subtract
             )

@@ -23,6 +23,7 @@ WORDS_PER_PASS = K_PASS // 2
 TILES_PER_BANK = 2
 BANKS_PER_PASS = N_TILES // TILES_PER_BANK
 
+WORDS_PER_HALF = WORDS_PER_PASS // 2
 PASSES_PER_LOAD = 2
 K_LOAD = PASSES_PER_LOAD * K_PASS
 LOADS = K // K_LOAD
@@ -64,16 +65,16 @@ def tile_gaussianmlpbasislayer_pb_k_kernel(tc, xf, mean, var, grad_out, out):
                 ks = slice(piece * n * K_PASS, (piece + 1) * n * K_PASS)
                 k_rows = slice((i * PASSES_PER_LOAD + piece * n) * K_PASS, (i * PASSES_PER_LOAD + (piece + 1) * n) * K_PASS)
                 nc.sync.dma_start(
-                    out=var_sb[i][:, cs].rearrange("p c j d -> p c (j d)"),
-                    in_=var[k_rows, :].rearrange("(c p j) d -> p c (j d)", p=P, j=PACK),
+                    out=var_sb[i][:, cs].rearrange("p c (u e) d -> p (c u) (e d)", e=2),
+                    in_=var[k_rows, :].rearrange("(h p e) d -> p h (e d)", p=P, e=2),
                 )
                 nc.sync.dma_start(
                     out=g_sb[i][:, :, ks],
                     in_=grad_out[:, k_rows].rearrange("(a p) k -> p a k", p=P),
                 )
                 nc.sync.dma_start(
-                    out=mean_sb[i][:, cs].rearrange("p c j d -> p c (j d)"),
-                    in_=mean[k_rows, :].rearrange("(c p j) d -> p c (j d)", p=P, j=PACK),
+                    out=mean_sb[i][:, cs].rearrange("p c (u e) d -> p (c u) (e d)", e=2),
+                    in_=mean[k_rows, :].rearrange("(h p e) d -> p h (e d)", p=P, e=2),
                 )
 
         def transpose_g(c):
@@ -83,13 +84,10 @@ def tile_gaussianmlpbasislayer_pb_k_kernel(tc, xf, mean, var, grad_out, out):
                 xt[c, h] = xt_pool.tile([P, TILES_PER_BANK, 2, P], F32, name="xt")
                 for b in range(TILES_PER_BANK):
                     for u in range(2):
+                        first = ci * WORDS_PER_PASS + u * WORDS_PER_HALF
                         nc.tensor.transpose(
                             out=xt[c, h][:, b, u, :],
-                            in_=g_words[
-                                :,
-                                h * TILES_PER_BANK + b,
-                                ci * WORDS_PER_PASS + u : (ci + 1) * WORDS_PER_PASS : 2,
-                            ],
+                            in_=g_words[:, h * TILES_PER_BANK + b, first : first + WORDS_PER_HALF],
                             identity=identity[:],
                         )
 
@@ -109,7 +107,7 @@ def tile_gaussianmlpbasislayer_pb_k_kernel(tc, xf, mean, var, grad_out, out):
             rsqrt_var[c] = pairs.tile([P, D, PACK], F32, name="rsqrt_var")
             nc.scalar.activation(
                 out=rsqrt_var[c][:],
-                in_=var_sb[i][:, ci].rearrange("p j d -> p d j"),
+                in_=var_sb[i][:, ci].rearrange("p t d -> p d t"),
                 func=ACT.Abs_reciprocal_sqrt,
             )
 
@@ -122,7 +120,7 @@ def tile_gaussianmlpbasislayer_pb_k_kernel(tc, xf, mean, var, grad_out, out):
             w_bf = pairs.tile([P, 2, D, PACK], BF16, name="w_bf", align_bytes=64)
             nc.vector.tensor_tensor(
                 out=w_bf[:, 0],
-                in0=mean_sb[i][:, ci].rearrange("p j d -> p d j"),
+                in0=mean_sb[i][:, ci].rearrange("p t d -> p d t"),
                 in1=inv_var[c][:],
                 op=ALU.mult,
             )

@@ -104,16 +104,20 @@ def tile_gaussianmlpbasislayer_pb_k_kernel(tc, xf, mean, var, grad_out, out):
 
         def take_rsqrt(c):
             i, ci = divmod(c, PASSES_PER_LOAD)
-            rsqrt_var[c] = pairs.tile([P, D, PACK], F32, name="rsqrt_var")
+            rsqrt_var[c] = pairs.tile([P, 2, D, 2], F32, name="rsqrt_var")
             nc.scalar.activation(
                 out=rsqrt_var[c][:],
-                in_=var_sb[i][:, ci].rearrange("p t d -> p d t"),
+                in_=var_sb[i][:, ci].rearrange("p (u e) d -> p u d e", e=2),
                 func=ACT.Abs_reciprocal_sqrt,
             )
 
         def square(c):
             inv_var[c] = triples.tile([P, D, PACK], F32, name="inv_var")
-            nc.scalar.activation(out=inv_var[c][:], in_=rsqrt_var[c][:], func=ACT.Square)
+            nc.scalar.activation(
+                out=inv_var[c][:].rearrange("p d (u e) -> p d u e", e=2),
+                in_=rsqrt_var[c][:].rearrange("p u d e -> p d u e"),
+                func=ACT.Square,
+            )
 
         def quantise(c):
             i, ci = divmod(c, PASSES_PER_LOAD)

@@ -32,6 +32,8 @@ LOADS_AHEAD = LOAD_BUFS - 1
 
 VECTOR_EVERY = 4
 
+RUN = 4
+
 FLOPS = 2 * NT * K * (2 * D)
 
 
@@ -104,31 +106,29 @@ def tile_gaussianmlpbasislayer_pb_k_kernel(tc, xf, mean, var, grad_out, out):
 
         def take_rsqrt(c):
             i, ci = divmod(c, PASSES_PER_LOAD)
-            rsqrt_var[c] = pairs.tile([P, 2, D, 2], F32, name="rsqrt_var")
+            rsqrt_var[c] = pairs.tile([P, D // RUN, PACK, RUN], F32, name="rsqrt_var")
             nc.scalar.activation(
                 out=rsqrt_var[c][:],
-                in_=var_sb[i][:, ci].rearrange("p (u e) d -> p u d e", e=2),
+                in_=var_sb[i][:, ci].rearrange("p t (b i) -> p b t i", i=RUN),
                 func=ACT.Abs_reciprocal_sqrt,
             )
 
         def square(c):
-            inv_var[c] = triples.tile([P, D, PACK], F32, name="inv_var")
-            nc.scalar.activation(
-                out=inv_var[c][:].rearrange("p d (u e) -> p d u e", e=2),
-                in_=rsqrt_var[c][:].rearrange("p u d e -> p d u e"),
-                func=ACT.Square,
-            )
+            inv_var[c] = triples.tile([P, D // RUN, PACK, RUN], F32, name="inv_var")
+            nc.scalar.activation(out=inv_var[c][:], in_=rsqrt_var[c][:], func=ACT.Square)
 
         def quantise(c):
             i, ci = divmod(c, PASSES_PER_LOAD)
             w_bf = pairs.tile([P, 2, D, PACK], BF16, name="w_bf", align_bytes=64)
             nc.vector.tensor_tensor(
-                out=w_bf[:, 0],
-                in0=mean_sb[i][:, ci].rearrange("p t d -> p d t"),
+                out=w_bf[:, 0].rearrange("p (b i) t -> p b t i", i=RUN),
+                in0=mean_sb[i][:, ci].rearrange("p t (b i) -> p b t i", i=RUN),
                 in1=inv_var[c][:],
                 op=ALU.mult,
             )
-            nc.vector.tensor_copy(out=w_bf[:, 1], in_=inv_var[c][:])
+            nc.vector.tensor_copy(
+                out=w_bf[:, 1].rearrange("p (b i) t -> p b t i", i=RUN), in_=inv_var[c][:]
+            )
             g_codes[c] = triples.tile([P, NT], U32, name="g_codes", align_bytes=64)
             g_scales[c] = triples.tile([P, NT], U8, name="g_scales", align_bytes=64)
             nc.vector.quantize_mx(

@@ -22,7 +22,6 @@ PASSES = K // K_PASS
 WORDS_PER_PASS = K_PASS // 2
 TILES_PER_BANK = 2
 BANKS_PER_PASS = N_TILES // TILES_PER_BANK
-
 WORDS_PER_HALF = WORDS_PER_PASS // 2
 PASSES_PER_LOAD = 2
 K_LOAD = PASSES_PER_LOAD * K_PASS
@@ -30,11 +29,19 @@ LOADS = K // K_LOAD
 LOAD_BUFS = 4
 LOADS_AHEAD = LOAD_BUFS - 1
 
-VECTOR_EVERY = 4
+FLOPS = 2 * NT * K * (2 * D)
 
 RUN = 4
 
-FLOPS = 2 * NT * K * (2 * D)
+UNITS = (
+    [(c,) for c in range(2)]
+    + [(c, c + 1) for c in range(2, PASSES - 2, 2)]
+    + [(c,) for c in range(PASSES - 2, PASSES)]
+)
+
+
+def vector_empties(c, h):
+    return c < 2 or (h == 1 and c % 4 == 3 and c < PASSES - 2)
 
 
 def tile_gaussianmlpbasislayer_pb_k_kernel(tc, xf, mean, var, grad_out, out):
@@ -54,8 +61,12 @@ def tile_gaussianmlpbasislayer_pb_k_kernel(tc, xf, mean, var, grad_out, out):
         acc = [acc_pool.tile([P, 2 * D], F32, name="acc%d" % a) for a in range(N_TILES)]
 
         var_sb, mean_sb, g_sb = {}, {}, {}
-        rsqrt_var, inv_var, xt, g_bf = {}, {}, {}, {}
+        rsqrt_var, inv_var, xt, g_bf, w_bf = {}, {}, {}, {}, {}
         g_codes, g_scales, w_codes, w_scales = {}, {}, {}, {}
+        unit_of = {}
+        for j, unit in enumerate(UNITS):
+            for c in unit:
+                unit_of[c] = j
 
         def load(i, pieces):
             var_sb[i] = loads.tile([P, PASSES_PER_LOAD, PACK, D], BF16, name="var_sb")
@@ -94,65 +105,80 @@ def tile_gaussianmlpbasislayer_pb_k_kernel(tc, xf, mean, var, grad_out, out):
                         )
 
         def empty_bank(c, h):
-            if h == 0:
-                g_bf[c] = triples.tile([P, N_TILES, P, PACK], BF16, name="g_bf", align_bytes=64)
-            g_bf_words = g_bf[c][:].bitcast(F32)
-            dst = g_bf_words[:, h * TILES_PER_BANK : (h + 1) * TILES_PER_BANK]
+            j = unit_of[c]
+            if c == UNITS[j][0] and h == 0:
+                g_bf[j] = triples.tile([P, len(UNITS[j]), N_TILES, P, PACK], BF16, name="g_bf", align_bytes=64)
+            g_bf_words = g_bf[j][:].bitcast(F32)
+            dst = g_bf_words[:, c - UNITS[j][0], h * TILES_PER_BANK : (h + 1) * TILES_PER_BANK]
             src = xt[c, h][:].rearrange("p b u n -> p b n u")
-            if (c * BANKS_PER_PASS + h) % VECTOR_EVERY == VECTOR_EVERY - 1:
+            if vector_empties(c, h):
                 nc.vector.tensor_copy(out=dst, in_=src)
             else:
                 nc.scalar.copy(out=dst, in_=src)
 
-        def take_rsqrt(c):
-            i, ci = divmod(c, PASSES_PER_LOAD)
-            rsqrt_var[c] = pairs.tile([P, D // RUN, PACK, RUN], F32, name="rsqrt_var")
+        def take_rsqrt(j):
+            unit = UNITS[j]
+            i, first = divmod(unit[0], PASSES_PER_LOAD)
+            rsqrt_var[j] = pairs.tile([P, D // RUN, len(unit) * PACK, RUN], F32, name="rsqrt_var")
             nc.scalar.activation(
-                out=rsqrt_var[c][:],
-                in_=var_sb[i][:, ci].rearrange("p t (b i) -> p b t i", i=RUN),
+                out=rsqrt_var[j][:],
+                in_=var_sb[i][:, first : first + len(unit)].rearrange("p c t (b i) -> p b (c t) i", i=RUN),
                 func=ACT.Abs_reciprocal_sqrt,
             )
 
-        def square(c):
-            inv_var[c] = triples.tile([P, D // RUN, PACK, RUN], F32, name="inv_var")
-            nc.scalar.activation(out=inv_var[c][:], in_=rsqrt_var[c][:], func=ACT.Square)
+        def square(j):
+            inv_var[j] = triples.tile([P, D // RUN, len(UNITS[j]) * PACK, RUN], F32, name="inv_var")
+            nc.scalar.activation(out=inv_var[j][:], in_=rsqrt_var[j][:], func=ACT.Square)
 
-        def quantise(c):
+        def make_w(c):
+            j = unit_of[c]
             i, ci = divmod(c, PASSES_PER_LOAD)
-            w_bf = pairs.tile([P, 2, D, PACK], BF16, name="w_bf", align_bytes=64)
+            cc = c - UNITS[j][0]
+            if cc == 0:
+                w_bf[j] = pairs.tile([P, len(UNITS[j]), 2, D, PACK], BF16, name="w_bf", align_bytes=64)
+            inv_var_c = inv_var[j][:, :, cc * PACK : (cc + 1) * PACK, :]
             nc.vector.tensor_tensor(
-                out=w_bf[:, 0].rearrange("p (b i) t -> p b t i", i=RUN),
+                out=w_bf[j][:, cc, 0].rearrange("p (b i) t -> p b t i", i=RUN),
                 in0=mean_sb[i][:, ci].rearrange("p t (b i) -> p b t i", i=RUN),
-                in1=inv_var[c][:],
+                in1=inv_var_c,
                 op=ALU.mult,
             )
             nc.vector.tensor_copy(
-                out=w_bf[:, 1].rearrange("p (b i) t -> p b t i", i=RUN), in_=inv_var[c][:]
+                out=w_bf[j][:, cc, 1].rearrange("p (b i) t -> p b t i", i=RUN), in_=inv_var_c
             )
-            g_codes[c] = triples.tile([P, NT], U32, name="g_codes", align_bytes=64)
-            g_scales[c] = triples.tile([P, NT], U8, name="g_scales", align_bytes=64)
+
+        def quantise_g(j):
+            n = len(UNITS[j])
+            g_codes[j] = triples.tile([P, n * NT], U32, name="g_codes", align_bytes=64)
+            g_scales[j] = triples.tile([P, n * NT], U8, name="g_scales", align_bytes=64)
             nc.vector.quantize_mx(
-                out=g_codes[c][:].bitcast(E5M2_X4),
-                scales=g_scales[c][:],
-                in_=g_bf[c][:].rearrange("p a n t -> p (a n t)"),
+                out=g_codes[j][:].bitcast(E5M2_X4),
+                scales=g_scales[j][:],
+                in_=g_bf[j][:].rearrange("p c a n t -> p (c a n t)"),
             )
-            w_codes[c] = triples.tile([P, 2 * D], U32, name="w_codes", align_bytes=64)
-            w_scales[c] = triples.tile([P, 2 * D], U8, name="w_scales", align_bytes=64)
+
+        def quantise_w(j):
+            n = len(UNITS[j])
+            w_codes[j] = triples.tile([P, n * 2 * D], U32, name="w_codes", align_bytes=64)
+            w_scales[j] = triples.tile([P, n * 2 * D], U8, name="w_scales", align_bytes=64)
             nc.vector.quantize_mx(
-                out=w_codes[c][:].bitcast(E4M3_X4),
-                scales=w_scales[c][:],
-                in_=w_bf[:].rearrange("p h d t -> p (h d t)"),
+                out=w_codes[j][:].bitcast(E4M3_X4),
+                scales=w_scales[j][:],
+                in_=w_bf[j][:].rearrange("p c h d t -> p (c h d t)"),
             )
 
         def multiply(c):
+            j = unit_of[c]
+            first = (c - UNITS[j][0]) * NT
+            cols = slice(first, first + 2 * D)
             for a in range(N_TILES):
-                rows = slice(a * P, (a + 1) * P)
+                rows = slice(first + a * P, first + (a + 1) * P)
                 nc.tensor.matmul_mx(
                     out=acc[a][:],
-                    lhsT=g_codes[c][:, rows].bitcast(E5M2_X4),
-                    lhsT_scale=g_scales[c][:, rows],
-                    rhs=w_codes[c][:].bitcast(E4M3_X4),
-                    rhs_scale=w_scales[c][:],
+                    lhsT=g_codes[j][:, rows].bitcast(E5M2_X4),
+                    lhsT_scale=g_scales[j][:, rows],
+                    rhs=w_codes[j][:, cols].bitcast(E4M3_X4),
+                    rhs_scale=w_scales[j][:, cols],
                     start=(c == 0),
                     stop=(c == PASSES - 1),
                 )
@@ -163,32 +189,54 @@ def tile_gaussianmlpbasislayer_pb_k_kernel(tc, xf, mean, var, grad_out, out):
         x_sb = const.tile([P, N_TILES, D], BF16)
         nc.sync.dma_start(out=x_sb[:], in_=xf.rearrange("(a p) d -> p a d", p=P))
 
-        for step in range(-2, PASSES + 1):
-            if step >= 0 and step % PASSES_PER_LOAD == 0:
-                i = step // PASSES_PER_LOAD + LOADS_AHEAD
+        transpose_g(0)
+        transpose_g(1)
+        n_units = len(UNITS)
+        for j in range(-1, n_units + 1):
+            if 0 <= j < n_units and UNITS[j][0] % PASSES_PER_LOAD == 0:
+                i = UNITS[j][0] // PASSES_PER_LOAD + LOADS_AHEAD
                 if i < LOADS:
                     load(i, 1)
-            if step + 2 < PASSES:
-                transpose_g(step + 2)
-            if 0 <= step - 1:
-                multiply(step - 1)
-            if 0 <= step + 1 < PASSES:
-                square(step + 1)
-                empty_bank(step + 1, 0)
-            if step + 2 < PASSES:
-                take_rsqrt(step + 2)
-            if 0 <= step < PASSES:
-                quantise(step)
-            if 0 <= step + 1 < PASSES:
-                empty_bank(step + 1, 1)
+            if j + 1 < n_units:
+                take_rsqrt(j + 1)
+            passes = UNITS[j] if 0 <= j < n_units else ()
+            for c in passes:
+                make_w(c)
+            for c in passes[:1]:
+                empty_bank(c, 0)
+                empty_bank(c, 1)
+                if c + 2 < PASSES:
+                    transpose_g(c + 2)
+            if j + 1 < n_units:
+                square(j + 1)
+            if 0 <= j - 1:
+                quantise_g(j - 1)
+                for c in UNITS[j - 1]:
+                    multiply(c)
+            for c in passes[1:]:
+                empty_bank(c, 0)
+                empty_bank(c, 1)
+                if c + 2 < PASSES:
+                    transpose_g(c + 2)
+            if 0 <= j < n_units:
+                quantise_w(j)
 
-        for a in range(N_TILES):
-            x_b = pairs.tile([P, D], F32, name="x_b")
-            nc.vector.tensor_tensor(
-                out=x_b[:], in0=x_sb[:, a, :], in1=acc[a][:, D : 2 * D], op=ALU.mult
-            )
-            result = pairs.tile([P, D], F32, name="result")
-            nc.vector.tensor_tensor(
-                out=result[:], in0=acc[a][:, 0:D], in1=x_b[:], op=ALU.subtract
-            )
-            nc.sync.dma_start(out=out[a * P : (a + 1) * P, :], in_=result[:])
+        b_sb = const.tile([P, D], F32)
+        nc.scalar.copy(out=b_sb[:], in_=acc[0][:, D : 2 * D])
+        a_sb = const.tile([P, D], F32)
+        nc.scalar.copy(out=a_sb[:], in_=acc[0][:, 0:D])
+        x_b = [const.tile([P, D], F32, name="x_b%d" % a) for a in range(N_TILES)]
+        result = [const.tile([P, D], F32, name="result%d" % a) for a in range(N_TILES)]
+        nc.gpsimd.tensor_tensor(out=x_b[0][:], in0=x_sb[:, 0, :], in1=b_sb[:], op=ALU.mult)
+        nc.gpsimd.tensor_tensor(out=result[0][:], in0=a_sb[:], in1=x_b[0][:], op=ALU.subtract)
+        nc.sync.dma_start(out=out[0:P, :], in_=result[0][:])
+        for a in range(1, N_TILES + 1):
+            if a < N_TILES:
+                nc.vector.tensor_tensor(
+                    out=x_b[a][:], in0=x_sb[:, a, :], in1=acc[a][:, D : 2 * D], op=ALU.mult
+                )
+            if a - 1 >= 1:
+                nc.vector.tensor_tensor(
+                    out=result[a - 1][:], in0=acc[a - 1][:, 0:D], in1=x_b[a - 1][:], op=ALU.subtract
+                )
+                nc.sync.dma_start(out=out[(a - 1) * P : a * P, :], in_=result[a - 1][:])

@@ -41,7 +41,11 @@ UNITS = (
 
 
 def vector_empties(c, h):
-    return c < 2 or (h == 1 and c % 4 == 3 and c < PASSES - 2)
+    return c < 3 or (h == 1 and c % 4 == 3 and c < PASSES - 2)
+
+
+def scalar_rounds(c):
+    return c >= PASSES - 2
 
 
 def tile_gaussianmlpbasislayer_pb_k_kernel(tc, xf, mean, var, grad_out, out):
@@ -70,19 +74,25 @@ def tile_gaussianmlpbasislayer_pb_k_kernel(tc, xf, mean, var, grad_out, out):
 
         def load(i, pieces):
             var_sb[i] = loads.tile([P, PASSES_PER_LOAD, PACK, D], BF16, name="var_sb")
-            g_sb[i] = loads.tile([P, N_TILES, K_LOAD], BF16, name="g_sb")
+            if pieces == 1:
+                g_whole = loads.tile([P, N_TILES, K_LOAD], BF16, name="g_sb")
             mean_sb[i] = loads.tile([P, PASSES_PER_LOAD, PACK, D], BF16, name="mean_sb")
             n = PASSES_PER_LOAD // pieces
             for piece in range(pieces):
                 cs = slice(piece * n, (piece + 1) * n)
-                ks = slice(piece * n * K_PASS, (piece + 1) * n * K_PASS)
                 k_rows = slice((i * PASSES_PER_LOAD + piece * n) * K_PASS, (i * PASSES_PER_LOAD + (piece + 1) * n) * K_PASS)
                 nc.sync.dma_start(
                     out=var_sb[i][:, cs].rearrange("p c (u e) d -> p (c u) (e d)", e=2),
                     in_=var[k_rows, :].rearrange("(h p e) d -> p h (e d)", p=P, e=2),
                 )
+                if pieces == 1:
+                    g_piece = g_whole
+                else:
+                    g_piece = const.tile([P, N_TILES, n * K_PASS], BF16, name="g_piece%d" % piece)
+                for c in range(n):
+                    g_sb[i * PASSES_PER_LOAD + piece * n + c] = g_piece[:, :, c * K_PASS : (c + 1) * K_PASS]
                 nc.sync.dma_start(
-                    out=g_sb[i][:, :, ks],
+                    out=g_piece[:],
                     in_=grad_out[:, k_rows].rearrange("(a p) k -> p a k", p=P),
                 )
                 nc.sync.dma_start(
@@ -91,13 +101,12 @@ def tile_gaussianmlpbasislayer_pb_k_kernel(tc, xf, mean, var, grad_out, out):
                 )
 
         def transpose_g(c):
-            i, ci = divmod(c, PASSES_PER_LOAD)
-            g_words = g_sb[i][:].bitcast(F32)
+            g_words = g_sb[c].bitcast(F32)
             for h in range(BANKS_PER_PASS):
                 xt[c, h] = xt_pool.tile([P, TILES_PER_BANK, 2, P], F32, name="xt")
                 for b in range(TILES_PER_BANK):
                     for u in range(2):
-                        first = ci * WORDS_PER_PASS + u * WORDS_PER_HALF
+                        first = u * WORDS_PER_HALF
                         nc.tensor.transpose(
                             out=xt[c, h][:, b, u, :],
                             in_=g_words[:, h * TILES_PER_BANK + b, first : first + WORDS_PER_HALF],
@@ -134,8 +143,8 @@ def tile_gaussianmlpbasislayer_pb_k_kernel(tc, xf, mean, var, grad_out, out):
             j = unit_of[c]
             i, ci = divmod(c, PASSES_PER_LOAD)
             cc = c - UNITS[j][0]
-            if cc == 0:
-                w_bf[j] = pairs.tile([P, len(UNITS[j]), 2, D, PACK], BF16, name="w_bf", align_bytes=64)
+            if cc == 0 and not scalar_rounds(c):
+                w_bf[j] = triples.tile([P, len(UNITS[j]), 2, D, PACK], BF16, name="w_bf", align_bytes=64)
             inv_var_c = inv_var[j][:, :, cc * PACK : (cc + 1) * PACK, :]
             nc.vector.tensor_tensor(
                 out=w_bf[j][:, cc, 0].rearrange("p (b i) t -> p b t i", i=RUN),
@@ -143,8 +152,17 @@ def tile_gaussianmlpbasislayer_pb_k_kernel(tc, xf, mean, var, grad_out, out):
                 in1=inv_var_c,
                 op=ALU.mult,
             )
-            nc.vector.tensor_copy(
-                out=w_bf[j][:, cc, 1].rearrange("p (b i) t -> p b t i", i=RUN), in_=inv_var_c
+            if not scalar_rounds(c):
+                nc.vector.tensor_copy(
+                    out=w_bf[j][:, cc, 1].rearrange("p (b i) t -> p b t i", i=RUN), in_=inv_var_c
+                )
+
+        def round_on_scalar(j):
+            w_bf[j] = triples.tile([P, 1, 2, D, PACK], BF16, name="w_bf", align_bytes=64)
+            nc.scalar.activation(
+                out=w_bf[j][:, 0, 1].rearrange("p (b i) t -> p b t i", i=RUN),
+                in_=rsqrt_var[j][:],
+                func=ACT.Square,
             )
 
         def quantise_g(j):
@@ -200,15 +218,17 @@ def tile_gaussianmlpbasislayer_pb_k_kernel(tc, xf, mean, var, grad_out, out):
             if j + 1 < n_units:
                 take_rsqrt(j + 1)
             passes = UNITS[j] if 0 <= j < n_units else ()
-            for c in passes:
-                make_w(c)
             for c in passes[:1]:
                 empty_bank(c, 0)
                 empty_bank(c, 1)
                 if c + 2 < PASSES:
                     transpose_g(c + 2)
+            for c in passes:
+                make_w(c)
             if j + 1 < n_units:
                 square(j + 1)
+                if scalar_rounds(UNITS[j + 1][0]):
+                    round_on_scalar(j + 1)
             if 0 <= j - 1:
                 quantise_g(j - 1)
                 for c in UNITS[j - 1]:

from contextlib import ExitStack

import concourse.mybir as mybir
from concourse.masks import make_identity

F32 = mybir.dt.float32
BF16 = mybir.dt.bfloat16
U32 = mybir.dt.uint32
U8 = mybir.dt.uint8
E4M3_X4 = mybir.dt.float8_e4m3fn_x4
E5M2_X4 = mybir.dt.float8_e5m2_x4
ACT = mybir.ActivationFunctionType
ALU = mybir.AluOpType

P = 128
PACK = 4
K_PASS = P * PACK

NT, D, K = 512, 256, 16384
N_TILES = NT // P
PASSES = K // K_PASS
WORDS_PER_PASS = K_PASS // 2
TILES_PER_BANK = 2
BANKS_PER_PASS = N_TILES // TILES_PER_BANK
WORDS_PER_HALF = WORDS_PER_PASS // 2
PASSES_PER_LOAD = 2
K_LOAD = PASSES_PER_LOAD * K_PASS
LOADS = K // K_LOAD
LOAD_BUFS = 4
LOADS_AHEAD = LOAD_BUFS - 1

FLOPS = 2 * NT * K * (2 * D)

RUN = 4

UNITS = (
    [(c,) for c in range(2)]
    + [(c, c + 1) for c in range(2, PASSES - 2, 2)]
    + [(c,) for c in range(PASSES - 2, PASSES)]
)


def vector_empties(c, h):
    return c < 3 or (h == 1 and c % 4 == 3 and c < PASSES - 2)


def scalar_rounds(c):
    return c >= PASSES - 2


def tile_gaussianmlpbasislayer_pb_k_kernel(tc, xf, mean, var, grad_out, out):
    nc = tc.nc
    with ExitStack() as ctx:
        const = ctx.enter_context(tc.tile_pool(name="const", bufs=1))
        loads = ctx.enter_context(tc.tile_pool(name="loads", bufs=LOAD_BUFS))
        pairs = ctx.enter_context(tc.tile_pool(name="pairs", bufs=2))
        triples = ctx.enter_context(tc.tile_pool(name="triples", bufs=3))
        acc_pool = ctx.enter_context(tc.psum_pool(name="acc", bufs=1))
        xt_pool = ctx.enter_context(tc.psum_pool(name="xt", bufs=2 * BANKS_PER_PASS))
        ctx.enter_context(tc.manual_schedule())

        identity = const.tile([P, P], F32)
        make_identity(nc, identity[:])

        acc = [acc_pool.tile([P, 2 * D], F32, name="acc%d" % a) for a in range(N_TILES)]

        var_sb, mean_sb, g_sb = {}, {}, {}
        rsqrt_var, inv_var, xt, g_bf, w_bf = {}, {}, {}, {}, {}
        g_codes, g_scales, w_codes, w_scales = {}, {}, {}, {}
        unit_of = {}
        for j, unit in enumerate(UNITS):
            for c in unit:
                unit_of[c] = j

        def load(i, pieces):
            var_sb[i] = loads.tile([P, PASSES_PER_LOAD, PACK, D], BF16, name="var_sb")
            if pieces == 1:
                g_whole = loads.tile([P, N_TILES, K_LOAD], BF16, name="g_sb")
            mean_sb[i] = loads.tile([P, PASSES_PER_LOAD, PACK, D], BF16, name="mean_sb")
            n = PASSES_PER_LOAD // pieces
            for piece in range(pieces):
                cs = slice(piece * n, (piece + 1) * n)
                k_rows = slice((i * PASSES_PER_LOAD + piece * n) * K_PASS, (i * PASSES_PER_LOAD + (piece + 1) * n) * K_PASS)
                nc.sync.dma_start(
                    out=var_sb[i][:, cs].rearrange("p c (u e) d -> p (c u) (e d)", e=2),
                    in_=var[k_rows, :].rearrange("(h p e) d -> p h (e d)", p=P, e=2),
                )
                if pieces == 1:
                    g_piece = g_whole
                else:
                    g_piece = const.tile([P, N_TILES, n * K_PASS], BF16, name="g_piece%d" % piece)
                for c in range(n):
                    g_sb[i * PASSES_PER_LOAD + piece * n + c] = g_piece[:, :, c * K_PASS : (c + 1) * K_PASS]
                nc.sync.dma_start(
                    out=g_piece[:],
                    in_=grad_out[:, k_rows].rearrange("(a p) k -> p a k", p=P),
                )
                nc.sync.dma_start(
                    out=mean_sb[i][:, cs].rearrange("p c (u e) d -> p (c u) (e d)", e=2),
                    in_=mean[k_rows, :].rearrange("(h p e) d -> p h (e d)", p=P, e=2),
                )

        def transpose_g(c):
            g_words = g_sb[c].bitcast(F32)
            for h in range(BANKS_PER_PASS):
                xt[c, h] = xt_pool.tile([P, TILES_PER_BANK, 2, P], F32, name="xt")
                for b in range(TILES_PER_BANK):
                    for u in range(2):
                        first = u * WORDS_PER_HALF
                        nc.tensor.transpose(
                            out=xt[c, h][:, b, u, :],
                            in_=g_words[:, h * TILES_PER_BANK + b, first : first + WORDS_PER_HALF],
                            identity=identity[:],
                        )

        def empty_bank(c, h):
            j = unit_of[c]
            if c == UNITS[j][0] and h == 0:
                g_bf[j] = triples.tile([P, len(UNITS[j]), N_TILES, P, PACK], BF16, name="g_bf", align_bytes=64)
            g_bf_words = g_bf[j][:].bitcast(F32)
            dst = g_bf_words[:, c - UNITS[j][0], h * TILES_PER_BANK : (h + 1) * TILES_PER_BANK]
            src = xt[c, h][:].rearrange("p b u n -> p b n u")
            if vector_empties(c, h):
                nc.vector.tensor_copy(out=dst, in_=src)
            else:
                nc.scalar.copy(out=dst, in_=src)

        def take_rsqrt(j):
            unit = UNITS[j]
            i, first = divmod(unit[0], PASSES_PER_LOAD)
            rsqrt_var[j] = pairs.tile([P, D // RUN, len(unit) * PACK, RUN], F32, name="rsqrt_var")
            nc.scalar.activation(
                out=rsqrt_var[j][:],
                in_=var_sb[i][:, first : first + len(unit)].rearrange("p c t (b i) -> p b (c t) i", i=RUN),
                func=ACT.Abs_reciprocal_sqrt,
            )

        def square(j):
            inv_var[j] = triples.tile([P, D // RUN, len(UNITS[j]) * PACK, RUN], F32, name="inv_var")
            nc.scalar.activation(out=inv_var[j][:], in_=rsqrt_var[j][:], func=ACT.Square)

        def make_w(c):
            j = unit_of[c]
            i, ci = divmod(c, PASSES_PER_LOAD)
            cc = c - UNITS[j][0]
            if cc == 0 and not scalar_rounds(c):
                w_bf[j] = triples.tile([P, len(UNITS[j]), 2, D, PACK], BF16, name="w_bf", align_bytes=64)
            inv_var_c = inv_var[j][:, :, cc * PACK : (cc + 1) * PACK, :]
            nc.vector.tensor_tensor(
                out=w_bf[j][:, cc, 0].rearrange("p (b i) t -> p b t i", i=RUN),
                in0=mean_sb[i][:, ci].rearrange("p t (b i) -> p b t i", i=RUN),
                in1=inv_var_c,
                op=ALU.mult,
            )
            if not scalar_rounds(c):
                nc.vector.tensor_copy(
                    out=w_bf[j][:, cc, 1].rearrange("p (b i) t -> p b t i", i=RUN), in_=inv_var_c
                )

        def round_on_scalar(j):
            w_bf[j] = triples.tile([P, 1, 2, D, PACK], BF16, name="w_bf", align_bytes=64)
            nc.scalar.activation(
                out=w_bf[j][:, 0, 1].rearrange("p (b i) t -> p b t i", i=RUN),
                in_=rsqrt_var[j][:],
                func=ACT.Square,
            )

        def quantise_g(j):
            n = len(UNITS[j])
            g_codes[j] = triples.tile([P, n * NT], U32, name="g_codes", align_bytes=64)
            g_scales[j] = triples.tile([P, n * NT], U8, name="g_scales", align_bytes=64)
            nc.vector.quantize_mx(
                out=g_codes[j][:].bitcast(E5M2_X4),
                scales=g_scales[j][:],
                in_=g_bf[j][:].rearrange("p c a n t -> p (c a n t)"),
            )

        def quantise_w(j):
            n = len(UNITS[j])
            w_codes[j] = triples.tile([P, n * 2 * D], U32, name="w_codes", align_bytes=64)
            w_scales[j] = triples.tile([P, n * 2 * D], U8, name="w_scales", align_bytes=64)
            nc.vector.quantize_mx(
                out=w_codes[j][:].bitcast(E4M3_X4),
                scales=w_scales[j][:],
                in_=w_bf[j][:].rearrange("p c h d t -> p (c h d t)"),
            )

        def multiply(c):
            j = unit_of[c]
            first = (c - UNITS[j][0]) * NT
            cols = slice(first, first + 2 * D)
            for a in range(N_TILES):
                rows = slice(first + a * P, first + (a + 1) * P)
                nc.tensor.matmul_mx(
                    out=acc[a][:],
                    lhsT=g_codes[j][:, rows].bitcast(E5M2_X4),
                    lhsT_scale=g_scales[j][:, rows],
                    rhs=w_codes[j][:, cols].bitcast(E4M3_X4),
                    rhs_scale=w_scales[j][:, cols],
                    start=(c == 0),
                    stop=(c == PASSES - 1),
                )

        load(0, PASSES_PER_LOAD)
        for i in range(1, LOADS_AHEAD):
            load(i, 1)
        x_sb = const.tile([P, N_TILES, D], BF16)
        nc.sync.dma_start(out=x_sb[:], in_=xf.rearrange("(a p) d -> p a d", p=P))

        transpose_g(0)
        transpose_g(1)
        n_units = len(UNITS)
        for j in range(-1, n_units + 1):
            if 0 <= j < n_units and UNITS[j][0] % PASSES_PER_LOAD == 0:
                i = UNITS[j][0] // PASSES_PER_LOAD + LOADS_AHEAD
                if i < LOADS:
                    load(i, 1)
            if j + 1 < n_units:
                take_rsqrt(j + 1)
            passes = UNITS[j] if 0 <= j < n_units else ()
            for c in passes[:1]:
                empty_bank(c, 0)
                empty_bank(c, 1)
                if c + 2 < PASSES:
                    transpose_g(c + 2)
            for c in passes:
                make_w(c)
            if j + 1 < n_units:
                square(j + 1)
                if scalar_rounds(UNITS[j + 1][0]):
                    round_on_scalar(j + 1)
            if 0 <= j - 1:
                quantise_g(j - 1)
                for c in UNITS[j - 1]:
                    multiply(c)
            for c in passes[1:]:
                empty_bank(c, 0)
                empty_bank(c, 1)
                if c + 2 < PASSES:
                    transpose_g(c + 2)
            if 0 <= j < n_units:
                quantise_w(j)

        b_sb = const.tile([P, D], F32)
        nc.scalar.copy(out=b_sb[:], in_=acc[0][:, D : 2 * D])
        a_sb = const.tile([P, D], F32)
        nc.scalar.copy(out=a_sb[:], in_=acc[0][:, 0:D])
        x_b = [const.tile([P, D], F32, name="x_b%d" % a) for a in range(N_TILES)]
        result = [const.tile([P, D], F32, name="result%d" % a) for a in range(N_TILES)]
        nc.gpsimd.tensor_tensor(out=x_b[0][:], in0=x_sb[:, 0, :], in1=b_sb[:], op=ALU.mult)
        nc.gpsimd.tensor_tensor(out=result[0][:], in0=a_sb[:], in1=x_b[0][:], op=ALU.subtract)
        nc.sync.dma_start(out=out[0:P, :], in_=result[0][:])
        for a in range(1, N_TILES + 1):
            if a < N_TILES:
                nc.vector.tensor_tensor(
                    out=x_b[a][:], in0=x_sb[:, a, :], in1=acc[a][:, D : 2 * D], op=ALU.mult
                )
            if a - 1 >= 1:
                nc.vector.tensor_tensor(
                    out=result[a - 1][:], in0=acc[a - 1][:, 0:D], in1=x_b[a - 1][:], op=ALU.subtract
                )
                nc.sync.dma_start(out=out[(a - 1) * P : a * P, :], in_=result[a - 1][:])
